import numpy as np
import ml_dtypes


def mxq(x, axis, fmt="e4m3"):
    dtype, down = {"e4m3": (ml_dtypes.float8_e4m3fn, 7), "e5m2": (ml_dtypes.float8_e5m2, 14)}[fmt]
    v = np.moveaxis(np.asarray(x, np.float32).astype(ml_dtypes.bfloat16).astype(np.float64), axis, -1)
    blocks = v.reshape(v.shape[:-1] + (-1, 32))
    amax = np.abs(blocks).max(-1, keepdims=True)
    byte = np.maximum(np.where(amax > 0, np.frexp(amax)[1] - 1 + 127, 0) - down, 1)
    scale = np.exp2(byte - 127.0)
    codes = (blocks / scale).astype(np.float32).astype(dtype).astype(np.float64)
    return np.moveaxis((codes * scale).reshape(v.shape), -1, axis)


WIDE = False


def mx_kscale(k):
    if not WIDE:
        return np.ones(k)
    levels = np.array([10, -10, 5, -5, 0])
    a = np.random.permutation(np.resize(levels, k // 512 * 4)).reshape(k // 512, 4)
    idx = np.arange(k)
    return np.exp2(a[idx // 512, idx % 128 // 32])


BF16 = ml_dtypes.bfloat16


def bf(x):
    return np.asarray(x, np.float32).astype(BF16)


def f64(x):
    return np.asarray(x).astype(np.float64)


E2M1 = np.array([0.0, 0.5, 1.0, 1.5, 2.0, 3.0, 4.0, 6.0, -0.0, -0.5, -1.0, -1.5, -2.0, -3.0, -4.0, -6.0])


def pack_weight(w, fmt):
    k, n = w.shape
    w = f64(bf(w)).reshape(k // 32, 32, n)
    amax = np.abs(w).max(1)
    if fmt == "e4m3":
        byte = np.frexp(amax)[1] - 1 + 127 - 7
    else:
        mant, ex = np.frexp(amax / 6.0)
        byte = np.where(mant > 0.5, ex, ex - 1) + 127
    byte = np.clip(np.where(amax > 0, byte, 1), 1, 254)
    scaled = (w * np.exp2(127.0 - byte)[:, None, :]).reshape(k, n).astype(np.float32)
    by_word = np.ascontiguousarray(scaled.reshape(k // 512, 128, 4, n).transpose(0, 1, 3, 2))
    if fmt == "e4m3":
        words = by_word.astype(ml_dtypes.float8_e4m3fn).view(np.uint8)
    else:
        c = by_word.astype(ml_dtypes.float4_e2m1fn).view(np.uint8) & 0xF
        words = c[..., 0::2] | (c[..., 1::2] << 4)
    return np.ascontiguousarray(words), np.ascontiguousarray(byte.astype(np.uint8).reshape(k // 512, 16, n))


def unpack_weight(words, scales, fmt):
    g, p, n, _ = words.shape
    if fmt == "e4m3":
        vals = np.ascontiguousarray(words).view(ml_dtypes.float8_e4m3fn).astype(np.float64)
    else:
        nib = np.empty((g, p, n, 4), np.uint8)
        nib[..., 0::2] = words & 0xF
        nib[..., 1::2] = words >> 4
        vals = E2M1[nib]
    vals = vals * np.repeat(np.exp2(scales.astype(np.float64) - 127.0), 8, axis=1)[..., None]
    return vals.transpose(0, 1, 3, 2).reshape(g * 512, n)

def pack4(w):
    words, scales = pack_weight(w, "e2m1")
    return words.reshape(words.shape[0], 128, -1), scales


def unpack4(words, scales):
    return unpack_weight(words.reshape(words.shape[0], 128, -1, 2), scales, "e2m1")


B, S, HID, NH, HD, RD, RATIO = 1, 512, 512, 8, 128, 64, 4
THETA = 10000.0
HALF = RD // 2


def rope_tables(positions):
    inv_freq = 1.0 / THETA ** (np.arange(HALF) / HALF)
    ang = positions[:, None] * inv_freq[None, :]
    return np.cos(ang), np.sin(ang)


def rope_interleaved(x, cos, sin):
    nope, rope = x[..., :-RD], x[..., -RD:]
    pr = rope.reshape(rope.shape[:-1] + (HALF, 2))
    a, b = pr[..., 0], pr[..., 1]
    new = np.stack([a * cos - b * sin, a * sin + b * cos], axis=-1).reshape(rope.shape)
    return np.concatenate([nope, new], axis=-1)


def setup_inputs():
    s = mx_kscale(HID)
    hidden = bf(np.random.standard_normal((B, S, HID)) * s)
    wq_words, wq_scales = pack4(np.random.standard_normal((HID, NH * HD)) / np.sqrt(HID) / s[:, None])
    return {"hidden": hidden,
            "wq_words": wq_words,
            "wq_scales": wq_scales}


def reference(hidden, wq_words, wq_scales):
    q = mxq(f64(hidden), 2, "e4m3") @ unpack4(wq_words, wq_scales)
    q = q.reshape(B, S, NH, HD).transpose(0, 2, 1, 3)
    cq, sq = rope_tables(np.arange(S))
    return rope_interleaved(q, cq, sq)

@@ -1,0 +1,135 @@
+import math
+from contextlib import ExitStack
+
+import concourse.mybir as mybir
+from concourse.masks import make_identity
+
+F32 = mybir.dt.float32
+BF16 = mybir.dt.bfloat16
+I32 = mybir.dt.int32
+U32 = mybir.dt.uint32
+U8 = mybir.dt.uint8
+FP8X4 = mybir.dt.float8_e4m3fn_x4
+FP4X4 = mybir.dt.float4_e2m1fn_x4
+ALU = mybir.AluOpType
+ACT = mybir.ActivationFunctionType
+
+P = 128
+PACK = 4
+TOKENS = 512
+HID = P * PACK
+HEADS = 8
+HEAD_DIM = 128
+ROPE_DIM = 64
+NOPE_DIM = HEAD_DIM - ROPE_DIM
+PAIRS = ROPE_DIM // 2
+TILES = TOKENS // P
+THETA = 10000.0
+ROUND_MAGIC = 1.5 * 2.0**23
+
+FLOPS = 2 * TOKENS * HID * HEADS * HEAD_DIM
+
+
+def tile_deepseekv4attention_pb_s_kernel(tc, hidden, wq_words, wq_scales, out):
+    nc = tc.nc
+    with ExitStack() as stack:
+        keep = stack.enter_context(tc.tile_pool(name="keep", bufs=1))
+        prods = stack.enter_context(tc.tile_pool(name="prods", bufs=3))
+        results = stack.enter_context(tc.tile_pool(name="results", bufs=HEADS))
+        banks = stack.enter_context(tc.psum_pool(name="banks", bufs=8))
+
+        w_scales = keep.tile([P, HEADS * HEAD_DIM], U8, align_bytes=64)
+        nc.vector.memset(w_scales[:].bitcast(I32), 0)
+
+        x_sb = keep.tile([P, TILES, HID], BF16)
+        x_rows = hidden[0].rearrange("(p i) k -> p i k", i=TILES)
+        for first in range(0, TILES, 2):
+            nc.sync.dma_start(out=x_sb[:, first : first + 2, :], in_=x_rows[:, first : first + 2, :])
+        for quad in range(4):
+            nc.sync.dma_start(
+                out=w_scales[32 * quad : 32 * quad + 4, :].bitcast(I32),
+                in_=wq_scales[0, 4 * quad : 4 * quad + 4, :].bitcast(I32),
+            )
+        w_words = keep.tile([P, 2 * HEADS * HEAD_DIM], U8, align_bytes=64)
+        nc.sync.dma_start(out=w_words[:].bitcast(I32), in_=wq_words[0].bitcast(I32))
+
+        ident = keep.tile([P, P], F32)
+        make_identity(nc, ident[:])
+
+        token_int = keep.tile([P, TILES], I32)
+        nc.gpsimd.iota(token_int[:], pattern=[[1, TILES]], base=0, channel_multiplier=TILES)
+        token = keep.tile([P, TILES], F32)
+        nc.vector.tensor_copy(out=token[:], in_=token_int[:])
+        turns = keep.tile([P, 2, TILES, PAIRS], F32)
+        nc.vector.tensor_scalar_mul(
+            out=turns[:, 0, :, 0:1], in0=token[:].unsqueeze(2), scalar1=1.0 / (2.0 * math.pi)
+        )
+        for doubling in range(5):
+            w = 1 << doubling
+            nc.vector.tensor_scalar_mul(
+                out=turns[:, 0, :, w : 2 * w], in0=turns[:, 0, :, 0:w], scalar1=THETA ** (-w / PAIRS)
+            )
+        nc.vector.tensor_scalar_add(out=turns[:, 1], in0=turns[:, 0], scalar1=0.25)
+        whole = keep.tile([P, 2, TILES, PAIRS], F32)
+        nc.vector.tensor_scalar(
+            out=whole[:], in0=turns[:], scalar1=ROUND_MAGIC, scalar2=ROUND_MAGIC,
+            op0=ALU.add, op1=ALU.subtract,
+        )
+        part = keep.tile([P, 2, TILES, PAIRS], F32)
+        nc.vector.tensor_tensor(out=part[:], in0=turns[:], in1=whole[:], op=ALU.subtract)
+        table = keep.tile([P, 2, 2, TILES, PAIRS], F32)
+        nc.scalar.activation(out=table[:, 0, 0], in_=part[:, 1], func=ACT.Sin, scale=2.0 * math.pi)
+        nc.scalar.activation(out=table[:, 0, 1], in_=part[:, 0], func=ACT.Sin, scale=-2.0 * math.pi)
+        nc.scalar.activation(out=table[:, 1, 0], in_=part[:, 0], func=ACT.Sin, scale=2.0 * math.pi)
+        nc.scalar.activation(out=table[:, 1, 1], in_=part[:, 1], func=ACT.Sin, scale=2.0 * math.pi)
+
+        x_words = x_sb[:].bitcast(F32)
+        grouped = keep.tile([P, TILES, P, PACK], BF16, align_bytes=64)
+        grouped_words = grouped[:].bitcast(F32)
+        for i in range(TILES):
+            xt = banks.tile([P, 2, P], F32, tag="bank")
+            for u in range(2):
+                nc.tensor.transpose(xt[:, u, :], x_words[:, i, u : HID // 2 : 2], ident[:])
+            copy_out = nc.vector.tensor_copy if i % 2 == 0 else nc.scalar.copy
+            copy_out(out=grouped_words[:, i], in_=xt[:].rearrange("p u t -> p t u"))
+        x_codes = keep.tile([P, TILES, P], U32, align_bytes=64)
+        x_scales = keep.tile([P, TILES, P], U8, align_bytes=64)
+        for i in range(TILES):
+            nc.vector.quantize_mx(
+                out=x_codes[:, i, :].bitcast(FP8X4),
+                scales=x_scales[:, i, :],
+                in_=grouped[:, i].rearrange("p t c -> p (t c)"),
+            )
+
+        for h in range(HEADS):
+            acc = banks.tile([P, TILES, HEAD_DIM], F32, tag="bank")
+            for i in range(TILES):
+                nc.tensor.matmul_mx(
+                    out=acc[:, i, :],
+                    lhsT=x_codes[:, i, :].bitcast(FP8X4),
+                    lhsT_scale=x_scales[:, i, :],
+                    rhs=w_words[:, 2 * HEAD_DIM * h : 2 * HEAD_DIM * (h + 1)].bitcast(FP4X4),
+                    rhs_scale=w_scales[:, HEAD_DIM * h : HEAD_DIM * (h + 1)],
+                    start=True,
+                    stop=True,
+                )
+            prod = prods.tile([P, 2, 2, TILES, PAIRS], F32)
+            pairs_in = acc[:, :, NOPE_DIM:].rearrange("p i (j e) -> p i j e", e=2)
+            nc.vector.tensor_tensor(
+                out=prod[:].rearrange("p e r i j -> p r i j e"),
+                in0=pairs_in.unsqueeze(1).to_broadcast([P, 2, TILES, PAIRS, 2]),
+                in1=table[:].rearrange("p r e i j -> p r i j e"),
+                op=ALU.mult,
+            )
+            res = results.tile([P, TILES, HEAD_DIM], F32)
+            nc.scalar.copy(out=res[:, :, :NOPE_DIM], in_=acc[:, :, :NOPE_DIM])
+            nc.gpsimd.tensor_tensor(
+                out=res[:, :, NOPE_DIM:].rearrange("p i (j r) -> p i j r", r=2),
+                in0=prod[:, 0].rearrange("p r i j -> p i j r"),
+                in1=prod[:, 1].rearrange("p r i j -> p i j r"),
+                op=ALU.add,
+            )
+            nc.sync.dma_start(
+                out=out[0, h].rearrange("(p i) d -> p (i d)", i=TILES),
+                in_=res[:].rearrange("p i d -> p (i d)"),
+            )

@@ -34,17 +34,18 @@ def tile_deepseekv4attention_pb_s_kernel(tc, hidden, wq_words, wq_scales, out):
     nc = tc.nc
     with ExitStack() as stack:
         keep = stack.enter_context(tc.tile_pool(name="keep", bufs=1))
-        prods = stack.enter_context(tc.tile_pool(name="prods", bufs=3))
+        prods = stack.enter_context(tc.tile_pool(name="prods", bufs=4))
         results = stack.enter_context(tc.tile_pool(name="results", bufs=HEADS))
         banks = stack.enter_context(tc.psum_pool(name="banks", bufs=8))
+        stack.enter_context(tc.manual_schedule())
 
         w_scales = keep.tile([P, HEADS * HEAD_DIM], U8, align_bytes=64)
         nc.vector.memset(w_scales[:].bitcast(I32), 0)
 
         x_sb = keep.tile([P, TILES, HID], BF16)
         x_rows = hidden[0].rearrange("(p i) k -> p i k", i=TILES)
-        for first in range(0, TILES, 2):
-            nc.sync.dma_start(out=x_sb[:, first : first + 2, :], in_=x_rows[:, first : first + 2, :])
+        for first, last in ((0, 2), (2, 3), (3, 4)):
+            nc.sync.dma_start(out=x_sb[:, first:last, :], in_=x_rows[:, first:last, :])
         for quad in range(4):
             nc.sync.dma_start(
                 out=w_scales[32 * quad : 32 * quad + 4, :].bitcast(I32),
@@ -53,13 +54,13 @@ def tile_deepseekv4attention_pb_s_kernel(tc, hidden, wq_words, wq_scales, out):
         w_words = keep.tile([P, 2 * HEADS * HEAD_DIM], U8, align_bytes=64)
         nc.sync.dma_start(out=w_words[:].bitcast(I32), in_=wq_words[0].bitcast(I32))
 
+        token = keep.tile([P, TILES], F32)
+        nc.gpsimd.iota(
+            token[:], pattern=[[1, TILES]], base=0, channel_multiplier=TILES,
+            allow_small_or_imprecise_dtypes=True,
+        )
         ident = keep.tile([P, P], F32)
         make_identity(nc, ident[:])
-
-        token_int = keep.tile([P, TILES], I32)
-        nc.gpsimd.iota(token_int[:], pattern=[[1, TILES]], base=0, channel_multiplier=TILES)
-        token = keep.tile([P, TILES], F32)
-        nc.vector.tensor_copy(out=token[:], in_=token_int[:])
         turns = keep.tile([P, 2, TILES, PAIRS], F32)
         nc.vector.tensor_scalar_mul(
             out=turns[:, 0, :, 0:1], in0=token[:].unsqueeze(2), scalar1=1.0 / (2.0 * math.pi)
@@ -86,20 +87,25 @@ def tile_deepseekv4attention_pb_s_kernel(tc, hidden, wq_words, wq_scales, out):
         x_words = x_sb[:].bitcast(F32)
         grouped = keep.tile([P, TILES, P, PACK], BF16, align_bytes=64)
         grouped_words = grouped[:].bitcast(F32)
+        x_codes = keep.tile([P, TILES, P], U32, align_bytes=64)
+        x_scales = keep.tile([P, TILES, P], U8, align_bytes=64)
+
+        def quantise(i):
+            nc.vector.quantize_mx(
+                out=x_codes[:, i, :].bitcast(FP8X4),
+                scales=x_scales[:, i, :],
+                in_=grouped[:, i].rearrange("p t c -> p (t c)"),
+            )
+
         for i in range(TILES):
             xt = banks.tile([P, 2, P], F32, tag="bank")
             for u in range(2):
                 nc.tensor.transpose(xt[:, u, :], x_words[:, i, u : HID // 2 : 2], ident[:])
             copy_out = nc.vector.tensor_copy if i % 2 == 0 else nc.scalar.copy
             copy_out(out=grouped_words[:, i], in_=xt[:].rearrange("p u t -> p t u"))
-        x_codes = keep.tile([P, TILES, P], U32, align_bytes=64)
-        x_scales = keep.tile([P, TILES, P], U8, align_bytes=64)
-        for i in range(TILES):
-            nc.vector.quantize_mx(
-                out=x_codes[:, i, :].bitcast(FP8X4),
-                scales=x_scales[:, i, :],
-                in_=grouped[:, i].rearrange("p t c -> p (t c)"),
-            )
+            if i > 0:
+                quantise(i - 1)
+        quantise(TILES - 1)
 
         for h in range(HEADS):
             acc = banks.tile([P, TILES, HEAD_DIM], F32, tag="bank")
@@ -123,7 +129,8 @@ def tile_deepseekv4attention_pb_s_kernel(tc, hidden, wq_words, wq_scales, out):
             )
             res = results.tile([P, TILES, HEAD_DIM], F32)
             nc.scalar.copy(out=res[:, :, :NOPE_DIM], in_=acc[:, :, :NOPE_DIM])
-            nc.gpsimd.tensor_tensor(
+            adder = nc.vector if h % 4 == 3 else nc.gpsimd
+            adder.tensor_tensor(
                 out=res[:, :, NOPE_DIM:].rearrange("p i (j r) -> p i j r", r=2),
                 in0=prod[:, 0].rearrange("p r i j -> p i j r"),
                 in1=prod[:, 1].rearrange("p r i j -> p i j r"),

@@ -119,10 +119,10 @@ def tile_deepseekv4attention_pb_s_kernel(tc, hidden, wq_words, wq_scales, out):
                     start=True,
                     stop=True,
                 )
-            prod = prods.tile([P, 2, 2, TILES, PAIRS], F32)
+            prod = prods.tile([P, 2, TILES, PAIRS, 2], F32)
             pairs_in = acc[:, :, NOPE_DIM:].rearrange("p i (j e) -> p i j e", e=2)
             nc.vector.tensor_tensor(
-                out=prod[:].rearrange("p e r i j -> p r i j e"),
+                out=prod[:],
                 in0=pairs_in.unsqueeze(1).to_broadcast([P, 2, TILES, PAIRS, 2]),
                 in1=table[:].rearrange("p r e i j -> p r i j e"),
                 op=ALU.mult,
@@ -132,8 +132,8 @@ def tile_deepseekv4attention_pb_s_kernel(tc, hidden, wq_words, wq_scales, out):
             adder = nc.vector if h % 4 == 3 else nc.gpsimd
             adder.tensor_tensor(
                 out=res[:, :, NOPE_DIM:].rearrange("p i (j r) -> p i j r", r=2),
-                in0=prod[:, 0].rearrange("p r i j -> p i j r"),
-                in1=prod[:, 1].rearrange("p r i j -> p i j r"),
+                in0=prod[:, :, :, :, 0].rearrange("p r i j -> p i j r"),
+                in1=prod[:, :, :, :, 1].rearrange("p r i j -> p i j r"),
                 op=ALU.add,
             )
             nc.sync.dma_start(

@@ -34,7 +34,7 @@ def tile_deepseekv4attention_pb_s_kernel(tc, hidden, wq_words, wq_scales, out):
     nc = tc.nc
     with ExitStack() as stack:
         keep = stack.enter_context(tc.tile_pool(name="keep", bufs=1))
-        prods = stack.enter_context(tc.tile_pool(name="prods", bufs=4))
+        prods = stack.enter_context(tc.tile_pool(name="prods", bufs=HEADS))
         results = stack.enter_context(tc.tile_pool(name="results", bufs=HEADS))
         banks = stack.enter_context(tc.psum_pool(name="banks", bufs=8))
         stack.enter_context(tc.manual_schedule())
@@ -44,31 +44,41 @@ def tile_deepseekv4attention_pb_s_kernel(tc, hidden, wq_words, wq_scales, out):
 
         x_sb = keep.tile([P, TILES, HID], BF16)
         x_rows = hidden[0].rearrange("(p i) k -> p i k", i=TILES)
-        for first, last in ((0, 2), (2, 3), (3, 4)):
+        for first, last in ((0, 1), (1, 2), (2, 4)):
             nc.sync.dma_start(out=x_sb[:, first:last, :], in_=x_rows[:, first:last, :])
-        for quad in range(4):
-            nc.sync.dma_start(
-                out=w_scales[32 * quad : 32 * quad + 4, :].bitcast(I32),
-                in_=wq_scales[0, 4 * quad : 4 * quad + 4, :].bitcast(I32),
-            )
         w_words = keep.tile([P, 2 * HEADS * HEAD_DIM], U8, align_bytes=64)
-        nc.sync.dma_start(out=w_words[:].bitcast(I32), in_=wq_words[0].bitcast(I32))
+        half_cols = HEADS * HEAD_DIM // 2
+        for half in range(2):
+            cols = slice(half * half_cols, (half + 1) * half_cols)
+            for quad in range(4):
+                nc.sync.dma_start(
+                    out=w_scales[32 * quad : 32 * quad + 4, cols].bitcast(I32),
+                    in_=wq_scales[0, 4 * quad : 4 * quad + 4, cols].bitcast(I32),
+                )
+            word_bytes = slice(2 * half * half_cols, 2 * (half + 1) * half_cols)
+            nc.sync.dma_start(
+                out=w_words[:, word_bytes].bitcast(I32), in_=wq_words[0, :, word_bytes].bitcast(I32)
+            )
 
         token = keep.tile([P, TILES], F32)
         nc.gpsimd.iota(
             token[:], pattern=[[1, TILES]], base=0, channel_multiplier=TILES,
             allow_small_or_imprecise_dtypes=True,
         )
+        zeros = keep.tile([P, PAIRS], F32)
+        nc.gpsimd.memset(zeros[:], 0.0)
         ident = keep.tile([P, P], F32)
         make_identity(nc, ident[:])
+        step = THETA ** (-1.0 / PAIRS)
+        ratio = keep.tile([P, PAIRS], F32)
+        nc.vector.tensor_scalar_add(out=ratio[:], in0=zeros[:], scalar1=step)
+        before = keep.tile([P, TILES], F32)
+        nc.vector.tensor_scalar_mul(out=before[:], in0=token[:], scalar1=1.0 / (2.0 * math.pi * step))
         turns = keep.tile([P, 2, TILES, PAIRS], F32)
-        nc.vector.tensor_scalar_mul(
-            out=turns[:, 0, :, 0:1], in0=token[:].unsqueeze(2), scalar1=1.0 / (2.0 * math.pi)
-        )
-        for doubling in range(5):
-            w = 1 << doubling
-            nc.vector.tensor_scalar_mul(
-                out=turns[:, 0, :, w : 2 * w], in0=turns[:, 0, :, 0:w], scalar1=THETA ** (-w / PAIRS)
+        for i in range(TILES):
+            nc.vector.tensor_tensor_scan(
+                out=turns[:, 0, i, :], data0=ratio[:], data1=zeros[:], initial=before[:, i : i + 1],
+                op0=ALU.mult, op1=ALU.add,
             )
         nc.vector.tensor_scalar_add(out=turns[:, 1], in0=turns[:, 0], scalar1=0.25)
         whole = keep.tile([P, 2, TILES, PAIRS], F32)
@@ -107,8 +117,13 @@ def tile_deepseekv4attention_pb_s_kernel(tc, hidden, wq_words, wq_scales, out):
                 quantise(i - 1)
         quantise(TILES - 1)
 
-        for h in range(HEADS):
-            acc = banks.tile([P, TILES, HEAD_DIM], F32, tag="bank")
+        accs = {}
+        prod_of = {}
+        res_of = {}
+
+        def project(h):
+            acc = banks.tile([P, TILES, HEAD_DIM], F32, tag="bank", name="acc")
+            accs[h] = acc
             for i in range(TILES):
                 nc.tensor.matmul_mx(
                     out=acc[:, i, :],
@@ -119,24 +134,56 @@ def tile_deepseekv4attention_pb_s_kernel(tc, hidden, wq_words, wq_scales, out):
                     start=True,
                     stop=True,
                 )
-            prod = prods.tile([P, 2, TILES, PAIRS, 2], F32)
-            pairs_in = acc[:, :, NOPE_DIM:].rearrange("p i (j e) -> p i j e", e=2)
+
+        def multiply(h):
+            prod = prods.tile([P, 2, TILES, PAIRS, 2], F32, name="prod")
+            prod_of[h] = prod
+            pairs_in = accs[h][:, :, NOPE_DIM:].rearrange("p i (j e) -> p i j e", e=2)
             nc.vector.tensor_tensor(
                 out=prod[:],
                 in0=pairs_in.unsqueeze(1).to_broadcast([P, 2, TILES, PAIRS, 2]),
                 in1=table[:].rearrange("p r e i j -> p r i j e"),
                 op=ALU.mult,
             )
-            res = results.tile([P, TILES, HEAD_DIM], F32)
-            nc.scalar.copy(out=res[:, :, :NOPE_DIM], in_=acc[:, :, :NOPE_DIM])
-            adder = nc.vector if h % 4 == 3 else nc.gpsimd
-            adder.tensor_tensor(
-                out=res[:, :, NOPE_DIM:].rearrange("p i (j r) -> p i j r", r=2),
-                in0=prod[:, :, :, :, 0].rearrange("p r i j -> p i j r"),
-                in1=prod[:, :, :, :, 1].rearrange("p r i j -> p i j r"),
+            res = results.tile([P, TILES, HEAD_DIM], F32, name="res")
+            res_of[h] = res
+            nc.scalar.copy(out=res[:, :, :NOPE_DIM], in_=accs[h][:, :, :NOPE_DIM])
+
+        def rotated(h):
+            return res_of[h][:, :, NOPE_DIM:].rearrange("p i (j r) -> p i j r", r=2)
+
+        def add_two_inputs(engine, h):
+            engine.tensor_tensor(
+                out=rotated(h),
+                in0=prod_of[h][:, :, :, :, 0].rearrange("p r i j -> p i j r"),
+                in1=prod_of[h][:, :, :, :, 1].rearrange("p r i j -> p i j r"),
                 op=ALU.add,
             )
-            nc.sync.dma_start(
+
+        def store(queue, h):
+            queue.dma_start(
                 out=out[0, h].rearrange("(p i) d -> p (i d)", i=TILES),
-                in_=res[:].rearrange("p i d -> p (i d)"),
+                in_=res_of[h][:].rearrange("p i d -> p (i d)"),
             )
+
+        for h in range(HEADS):
+            project(h)
+        for h in (0, 1, 2):
+            multiply(h)
+            add_two_inputs(nc.gpsimd, h)
+            store(nc.sync, h)
+        multiply(3)
+        add_two_inputs(nc.vector, 3)
+        store(nc.sync, 3)
+        multiply(4)
+        add_two_inputs(nc.gpsimd, 4)
+        store(nc.sync, 4)
+        multiply(5)
+        add_two_inputs(nc.gpsimd, 5)
+        multiply(6)
+        add_two_inputs(nc.vector, 6)
+        store(nc.sync, 6)
+        store(nc.sync, 5)
+        multiply(7)
+        add_two_inputs(nc.vector, 7)
+        store(nc.sync, 7)

@@ -168,22 +168,12 @@ def tile_deepseekv4attention_pb_s_kernel(tc, hidden, wq_words, wq_scales, out):
 
         for h in range(HEADS):
             project(h)
-        for h in (0, 1, 2):
+        for h in range(5):
             multiply(h)
             add_two_inputs(nc.gpsimd, h)
             store(nc.sync, h)
-        multiply(3)
-        add_two_inputs(nc.vector, 3)
-        store(nc.sync, 3)
-        multiply(4)
-        add_two_inputs(nc.gpsimd, 4)
-        store(nc.sync, 4)
-        multiply(5)
-        add_two_inputs(nc.gpsimd, 5)
-        multiply(6)
-        add_two_inputs(nc.vector, 6)
-        store(nc.sync, 6)
-        store(nc.sync, 5)
-        multiply(7)
-        add_two_inputs(nc.vector, 7)
-        store(nc.sync, 7)
+        for h in (5, 6, 7):
+            multiply(h)
+        for h in (5, 6, 7):
+            add_two_inputs(nc.vector, h)
+            store(nc.sync, h)

@@ -123,10 +123,11 @@ def tile_deepseekv4attention_pb_s_kernel(tc, hidden, wq_words, wq_scales, out):
 
         def project(h):
             acc = banks.tile([P, TILES, HEAD_DIM], F32, tag="bank", name="acc")
-            accs[h] = acc
+            late = banks.tile([P, 1, HEAD_DIM], F32, tag="bank", name="late") if h == 0 else acc[:, TILES - 1 :, :]
+            accs[h] = (acc, late)
             for i in range(TILES):
                 nc.tensor.matmul_mx(
-                    out=acc[:, i, :],
+                    out=acc[:, i, :] if i < TILES - 1 else late[:, 0, :],
                     lhsT=x_codes[:, i, :].bitcast(FP8X4),
                     lhsT_scale=x_scales[:, i, :],
                     rhs=w_words[:, 2 * HEAD_DIM * h : 2 * HEAD_DIM * (h + 1)].bitcast(FP4X4),
@@ -135,19 +136,25 @@ def tile_deepseekv4attention_pb_s_kernel(tc, hidden, wq_words, wq_scales, out):
                     stop=True,
                 )
 
-        def multiply(h):
-            prod = prods.tile([P, 2, TILES, PAIRS, 2], F32, name="prod")
-            prod_of[h] = prod
-            pairs_in = accs[h][:, :, NOPE_DIM:].rearrange("p i (j e) -> p i j e", e=2)
+        def multiply_tiles(h, bank, first, last):
+            pairs_in = bank[:, :, NOPE_DIM:].rearrange("p i (j e) -> p i j e", e=2)
             nc.vector.tensor_tensor(
-                out=prod[:],
-                in0=pairs_in.unsqueeze(1).to_broadcast([P, 2, TILES, PAIRS, 2]),
-                in1=table[:].rearrange("p r e i j -> p r i j e"),
+                out=prod_of[h][:, :, first:last],
+                in0=pairs_in.unsqueeze(1).to_broadcast([P, 2, last - first, PAIRS, 2]),
+                in1=table[:, :, :, first:last, :].rearrange("p r e i j -> p r i j e"),
                 op=ALU.mult,
             )
-            res = results.tile([P, TILES, HEAD_DIM], F32, name="res")
-            res_of[h] = res
-            nc.scalar.copy(out=res[:, :, :NOPE_DIM], in_=accs[h][:, :, :NOPE_DIM])
+            nc.scalar.copy(out=res_of[h][:, first:last, :NOPE_DIM], in_=bank[:, :, :NOPE_DIM])
+
+        def multiply(h):
+            prod_of[h] = prods.tile([P, 2, TILES, PAIRS, 2], F32, name="prod")
+            res_of[h] = results.tile([P, TILES, HEAD_DIM], F32, name="res")
+            acc, late = accs[h]
+            if h == 0:
+                multiply_tiles(h, acc[:, : TILES - 1, :], 0, TILES - 1)
+                multiply_tiles(h, late[:], TILES - 1, TILES)
+            else:
+                multiply_tiles(h, acc[:], 0, TILES)
 
         def rotated(h):
             return res_of[h][:, :, NOPE_DIM:].rearrange("p i (j r) -> p i j r", r=2)
@@ -166,10 +173,12 @@ def tile_deepseekv4attention_pb_s_kernel(tc, hidden, wq_words, wq_scales, out):
                 in_=res_of[h][:].rearrange("p i d -> p (i d)"),
             )
 
-        for h in range(HEADS):
+        for h in range(HEADS - 1):
             project(h)
         for h in range(5):
             multiply(h)
+            if h == 0:
+                project(HEADS - 1)
             add_two_inputs(nc.gpsimd, h)
             store(nc.sync, h)
         for h in (5, 6, 7):

@@ -27,6 +27,8 @@ TILES = TOKENS // P
 THETA = 10000.0
 ROUND_MAGIC = 1.5 * 2.0**23
 
+EARLY_HEADS = 2
+
 FLOPS = 2 * TOKENS * HID * HEADS * HEAD_DIM
 
 
@@ -121,20 +123,27 @@ def tile_deepseekv4attention_pb_s_kernel(tc, hidden, wq_words, wq_scales, out):
         prod_of = {}
         res_of = {}
 
-        def project(h):
+        def take_banks(h):
             acc = banks.tile([P, TILES, HEAD_DIM], F32, tag="bank", name="acc")
             late = banks.tile([P, 1, HEAD_DIM], F32, tag="bank", name="late") if h == 0 else acc[:, TILES - 1 :, :]
             accs[h] = (acc, late)
+
+        def project_tile(h, i):
+            acc, late = accs[h]
+            nc.tensor.matmul_mx(
+                out=acc[:, i, :] if i < TILES - 1 else late[:, 0, :],
+                lhsT=x_codes[:, i, :].bitcast(FP8X4),
+                lhsT_scale=x_scales[:, i, :],
+                rhs=w_words[:, 2 * HEAD_DIM * h : 2 * HEAD_DIM * (h + 1)].bitcast(FP4X4),
+                rhs_scale=w_scales[:, HEAD_DIM * h : HEAD_DIM * (h + 1)],
+                start=True,
+                stop=True,
+            )
+
+        def project(h):
+            take_banks(h)
             for i in range(TILES):
-                nc.tensor.matmul_mx(
-                    out=acc[:, i, :] if i < TILES - 1 else late[:, 0, :],
-                    lhsT=x_codes[:, i, :].bitcast(FP8X4),
-                    lhsT_scale=x_scales[:, i, :],
-                    rhs=w_words[:, 2 * HEAD_DIM * h : 2 * HEAD_DIM * (h + 1)].bitcast(FP4X4),
-                    rhs_scale=w_scales[:, HEAD_DIM * h : HEAD_DIM * (h + 1)],
-                    start=True,
-                    stop=True,
-                )
+                project_tile(h, i)
 
         def multiply_tiles(h, bank, first, last):
             pairs_in = bank[:, :, NOPE_DIM:].rearrange("p i (j e) -> p i j e", e=2)
@@ -173,7 +182,12 @@ def tile_deepseekv4attention_pb_s_kernel(tc, hidden, wq_words, wq_scales, out):
                 in_=res_of[h][:].rearrange("p i d -> p (i d)"),
             )
 
-        for h in range(HEADS - 1):
+        for h in range(EARLY_HEADS):
+            take_banks(h)
+        for i in range(TILES):
+            for h in range(EARLY_HEADS):
+                project_tile(h, i)
+        for h in range(EARLY_HEADS, HEADS - 1):
             project(h)
         for h in range(5):
             multiply(h)

@@ -113,7 +113,7 @@ def tile_deepseekv4attention_pb_s_kernel(tc, hidden, wq_words, wq_scales, out):
             xt = banks.tile([P, 2, P], F32, tag="bank")
             for u in range(2):
                 nc.tensor.transpose(xt[:, u, :], x_words[:, i, u : HID // 2 : 2], ident[:])
-            copy_out = nc.vector.tensor_copy if i % 2 == 0 else nc.scalar.copy
+            copy_out = nc.vector.tensor_copy if i < TILES // 2 else nc.scalar.copy
             copy_out(out=grouped_words[:, i], in_=xt[:].rearrange("p u t -> p t u"))
             if i > 0:
                 quantise(i - 1)

@@ -189,14 +189,28 @@ def tile_deepseekv4attention_pb_s_kernel(tc, hidden, wq_words, wq_scales, out):
                 project_tile(h, i)
         for h in range(EARLY_HEADS, HEADS - 1):
             project(h)
+        def add_by_reduce(h):
+            nc.vector.tensor_reduce(
+                out=rotated(h),
+                in_=prod_of[h][:].rearrange("p r i j e -> p i j r e"),
+                axis=mybir.AxisListType.X,
+                op=ALU.add,
+            )
+
         for h in range(5):
             multiply(h)
             if h == 0:
                 project(HEADS - 1)
             add_two_inputs(nc.gpsimd, h)
-            store(nc.sync, h)
-        for h in (5, 6, 7):
-            multiply(h)
-        for h in (5, 6, 7):
-            add_two_inputs(nc.vector, h)
-            store(nc.sync, h)
+            if h < 4:
+                store(nc.sync, h)
+        multiply(5)
+        add_by_reduce(5)
+        store(nc.sync, 5)
+        store(nc.sync, 4)
+        multiply(6)
+        add_two_inputs(nc.gpsimd, 6)
+        store(nc.sync, 6)
+        multiply(7)
+        add_two_inputs(nc.vector, 7)
+        store(nc.sync, 7)

import math
from contextlib import ExitStack

import concourse.mybir as mybir
from concourse.masks import make_identity

F32 = mybir.dt.float32
BF16 = mybir.dt.bfloat16
I32 = mybir.dt.int32
U32 = mybir.dt.uint32
U8 = mybir.dt.uint8
FP8X4 = mybir.dt.float8_e4m3fn_x4
FP4X4 = mybir.dt.float4_e2m1fn_x4
ALU = mybir.AluOpType
ACT = mybir.ActivationFunctionType

P = 128
PACK = 4
TOKENS = 512
HID = P * PACK
HEADS = 8
HEAD_DIM = 128
ROPE_DIM = 64
NOPE_DIM = HEAD_DIM - ROPE_DIM
PAIRS = ROPE_DIM // 2
TILES = TOKENS // P
THETA = 10000.0
ROUND_MAGIC = 1.5 * 2.0**23

EARLY_HEADS = 2

FLOPS = 2 * TOKENS * HID * HEADS * HEAD_DIM


def tile_deepseekv4attention_pb_s_kernel(tc, hidden, wq_words, wq_scales, out):
    nc = tc.nc
    with ExitStack() as stack:
        keep = stack.enter_context(tc.tile_pool(name="keep", bufs=1))
        prods = stack.enter_context(tc.tile_pool(name="prods", bufs=HEADS))
        results = stack.enter_context(tc.tile_pool(name="results", bufs=HEADS))
        banks = stack.enter_context(tc.psum_pool(name="banks", bufs=8))
        stack.enter_context(tc.manual_schedule())

        w_scales = keep.tile([P, HEADS * HEAD_DIM], U8, align_bytes=64)
        nc.vector.memset(w_scales[:].bitcast(I32), 0)

        x_sb = keep.tile([P, TILES, HID], BF16)
        x_rows = hidden[0].rearrange("(p i) k -> p i k", i=TILES)
        for first, last in ((0, 1), (1, 2), (2, 4)):
            nc.sync.dma_start(out=x_sb[:, first:last, :], in_=x_rows[:, first:last, :])
        w_words = keep.tile([P, 2 * HEADS * HEAD_DIM], U8, align_bytes=64)
        half_cols = HEADS * HEAD_DIM // 2
        for half in range(2):
            cols = slice(half * half_cols, (half + 1) * half_cols)
            for quad in range(4):
                nc.sync.dma_start(
                    out=w_scales[32 * quad : 32 * quad + 4, cols].bitcast(I32),
                    in_=wq_scales[0, 4 * quad : 4 * quad + 4, cols].bitcast(I32),
                )
            word_bytes = slice(2 * half * half_cols, 2 * (half + 1) * half_cols)
            nc.sync.dma_start(
                out=w_words[:, word_bytes].bitcast(I32), in_=wq_words[0, :, word_bytes].bitcast(I32)
            )

        token = keep.tile([P, TILES], F32)
        nc.gpsimd.iota(
            token[:], pattern=[[1, TILES]], base=0, channel_multiplier=TILES,
            allow_small_or_imprecise_dtypes=True,
        )
        zeros = keep.tile([P, PAIRS], F32)
        nc.gpsimd.memset(zeros[:], 0.0)
        ident = keep.tile([P, P], F32)
        make_identity(nc, ident[:])
        step = THETA ** (-1.0 / PAIRS)
        ratio = keep.tile([P, PAIRS], F32)
        nc.vector.tensor_scalar_add(out=ratio[:], in0=zeros[:], scalar1=step)
        before = keep.tile([P, TILES], F32)
        nc.vector.tensor_scalar_mul(out=before[:], in0=token[:], scalar1=1.0 / (2.0 * math.pi * step))
        turns = keep.tile([P, 2, TILES, PAIRS], F32)
        for i in range(TILES):
            nc.vector.tensor_tensor_scan(
                out=turns[:, 0, i, :], data0=ratio[:], data1=zeros[:], initial=before[:, i : i + 1],
                op0=ALU.mult, op1=ALU.add,
            )
        nc.vector.tensor_scalar_add(out=turns[:, 1], in0=turns[:, 0], scalar1=0.25)
        whole = keep.tile([P, 2, TILES, PAIRS], F32)
        nc.vector.tensor_scalar(
            out=whole[:], in0=turns[:], scalar1=ROUND_MAGIC, scalar2=ROUND_MAGIC,
            op0=ALU.add, op1=ALU.subtract,
        )
        part = keep.tile([P, 2, TILES, PAIRS], F32)
        nc.vector.tensor_tensor(out=part[:], in0=turns[:], in1=whole[:], op=ALU.subtract)
        table = keep.tile([P, 2, 2, TILES, PAIRS], F32)
        nc.scalar.activation(out=table[:, 0, 0], in_=part[:, 1], func=ACT.Sin, scale=2.0 * math.pi)
        nc.scalar.activation(out=table[:, 0, 1], in_=part[:, 0], func=ACT.Sin, scale=-2.0 * math.pi)
        nc.scalar.activation(out=table[:, 1, 0], in_=part[:, 0], func=ACT.Sin, scale=2.0 * math.pi)
        nc.scalar.activation(out=table[:, 1, 1], in_=part[:, 1], func=ACT.Sin, scale=2.0 * math.pi)

        x_words = x_sb[:].bitcast(F32)
        grouped = keep.tile([P, TILES, P, PACK], BF16, align_bytes=64)
        grouped_words = grouped[:].bitcast(F32)
        x_codes = keep.tile([P, TILES, P], U32, align_bytes=64)
        x_scales = keep.tile([P, TILES, P], U8, align_bytes=64)

        def quantise(i):
            nc.vector.quantize_mx(
                out=x_codes[:, i, :].bitcast(FP8X4),
                scales=x_scales[:, i, :],
                in_=grouped[:, i].rearrange("p t c -> p (t c)"),
            )

        for i in range(TILES):
            xt = banks.tile([P, 2, P], F32, tag="bank")
            for u in range(2):
                nc.tensor.transpose(xt[:, u, :], x_words[:, i, u : HID // 2 : 2], ident[:])
            copy_out = nc.vector.tensor_copy if i < TILES // 2 else nc.scalar.copy
            copy_out(out=grouped_words[:, i], in_=xt[:].rearrange("p u t -> p t u"))
            if i > 0:
                quantise(i - 1)
        quantise(TILES - 1)

        accs = {}
        prod_of = {}
        res_of = {}

        def take_banks(h):
            acc = banks.tile([P, TILES, HEAD_DIM], F32, tag="bank", name="acc")
            late = banks.tile([P, 1, HEAD_DIM], F32, tag="bank", name="late") if h == 0 else acc[:, TILES - 1 :, :]
            accs[h] = (acc, late)

        def project_tile(h, i):
            acc, late = accs[h]
            nc.tensor.matmul_mx(
                out=acc[:, i, :] if i < TILES - 1 else late[:, 0, :],
                lhsT=x_codes[:, i, :].bitcast(FP8X4),
                lhsT_scale=x_scales[:, i, :],
                rhs=w_words[:, 2 * HEAD_DIM * h : 2 * HEAD_DIM * (h + 1)].bitcast(FP4X4),
                rhs_scale=w_scales[:, HEAD_DIM * h : HEAD_DIM * (h + 1)],
                start=True,
                stop=True,
            )

        def project(h):
            take_banks(h)
            for i in range(TILES):
                project_tile(h, i)

        def multiply_tiles(h, bank, first, last):
            pairs_in = bank[:, :, NOPE_DIM:].rearrange("p i (j e) -> p i j e", e=2)
            nc.vector.tensor_tensor(
                out=prod_of[h][:, :, first:last],
                in0=pairs_in.unsqueeze(1).to_broadcast([P, 2, last - first, PAIRS, 2]),
                in1=table[:, :, :, first:last, :].rearrange("p r e i j -> p r i j e"),
                op=ALU.mult,
            )
            nc.scalar.copy(out=res_of[h][:, first:last, :NOPE_DIM], in_=bank[:, :, :NOPE_DIM])

        def multiply(h):
            prod_of[h] = prods.tile([P, 2, TILES, PAIRS, 2], F32, name="prod")
            res_of[h] = results.tile([P, TILES, HEAD_DIM], F32, name="res")
            acc, late = accs[h]
            if h == 0:
                multiply_tiles(h, acc[:, : TILES - 1, :], 0, TILES - 1)
                multiply_tiles(h, late[:], TILES - 1, TILES)
            else:
                multiply_tiles(h, acc[:], 0, TILES)

        def rotated(h):
            return res_of[h][:, :, NOPE_DIM:].rearrange("p i (j r) -> p i j r", r=2)

        def add_two_inputs(engine, h):
            engine.tensor_tensor(
                out=rotated(h),
                in0=prod_of[h][:, :, :, :, 0].rearrange("p r i j -> p i j r"),
                in1=prod_of[h][:, :, :, :, 1].rearrange("p r i j -> p i j r"),
                op=ALU.add,
            )

        def store(queue, h):
            queue.dma_start(
                out=out[0, h].rearrange("(p i) d -> p (i d)", i=TILES),
                in_=res_of[h][:].rearrange("p i d -> p (i d)"),
            )

        for h in range(EARLY_HEADS):
            take_banks(h)
        for i in range(TILES):
            for h in range(EARLY_HEADS):
                project_tile(h, i)
        for h in range(EARLY_HEADS, HEADS - 1):
            project(h)
        def add_by_reduce(h):
            nc.vector.tensor_reduce(
                out=rotated(h),
                in_=prod_of[h][:].rearrange("p r i j e -> p i j r e"),
                axis=mybir.AxisListType.X,
                op=ALU.add,
            )

        for h in range(5):
            multiply(h)
            if h == 0:
                project(HEADS - 1)
            add_two_inputs(nc.gpsimd, h)
            if h < 4:
                store(nc.sync, h)
        multiply(5)
        add_by_reduce(5)
        store(nc.sync, 5)
        store(nc.sync, 4)
        multiply(6)
        add_two_inputs(nc.gpsimd, 6)
        store(nc.sync, 6)
        multiply(7)
        add_two_inputs(nc.vector, 7)
        store(nc.sync, 7)
